import numpy as np
import ml_dtypes

BF16 = ml_dtypes.bfloat16


def bf(x):
    return np.asarray(x, np.float32).astype(BF16)


def f32(x):
    return np.asarray(x, np.float32)


def f64(x):
    return np.asarray(x).astype(np.float64)


def striped(idx):
    return np.tile(idx.reshape(-1, 16).T, (8, 1))


C, S, H, K, P, N = 1024, 1024, 512, 4, 4, 2048
GAMMA, XI, SPAN = -0.1, 1.1, 4.0


def soft_mask(u):
    return np.minimum(np.maximum((XI - GAMMA) / (1.0 + np.exp(-u)) + GAMMA, 0.0), 1.0)


def setup_inputs():
    weight = f32(np.random.standard_normal((C, S)))
    sparse_mask = f32(np.random.uniform(-SPAN, SPAN, (C, S)))
    s1 = f32(np.random.standard_normal((1, N)) / np.sqrt(K))
    s0 = f32(np.random.standard_normal((C, P)) / np.sqrt(P))
    rp = np.zeros((P, C, C), np.float32)
    for p in range(P):
        rp[p, np.random.permutation(C), np.arange(C)] = 1.0
    idx = np.concatenate([np.random.permutation(S)[:H] for _ in range(K)])
    return {"weight": weight, "sparse_mask": sparse_mask, "s1": s1, "s0": s0, "rp": bf(rp), "offs": striped(idx)}


def reference(weight, sparse_mask, s1, s0, rp, offs):
    idx = offs[:16].T.reshape(-1)
    sw = f64(weight) * soft_mask(f64(sparse_mask))
    v = (sw[:, idx] * f64(s1)).reshape(C, K, H).sum(axis=1)
    res = np.zeros((C, H))
    for p in range(P):
        res = res + f64(s0)[:, p:p + 1] * (f64(rp)[p].T @ v)
    return res

@@ -1,0 +1,102 @@
+import concourse.mybir as mybir
+
+F32 = mybir.dt.float32
+BF16 = mybir.dt.bfloat16
+U16 = mybir.dt.uint16
+ALU = mybir.AluOpType
+ACT = mybir.ActivationFunctionType
+
+P = 128
+C = 1024
+S = 1024
+H = 512
+K = 4
+NPERM = 4
+N = K * H
+CB = C // P
+RB = C // P
+GATHER = S
+FIRST_RB = 8 // NPERM
+
+FLOPS = 2 * NPERM * C * C * H
+
+
+def tile_permutatedsoftsparse_b_kernel(tc, weight, sparse_mask, s1, s0, rp, offs, out):
+    nc = tc.nc
+    with (
+        tc.tile_pool(name="held", bufs=1) as held,
+        tc.tile_pool(name="loads", bufs=3) as loads,
+        tc.tile_pool(name="work", bufs=2) as work,
+        tc.tile_pool(name="results", bufs=2) as results,
+        tc.psum_pool(name="psum", bufs=8) as psum,
+    ):
+        offsets = held.tile([P, N // 16], U16, name="offsets")
+        nc.sync.dma_start(offsets[:], offs)
+        s1_all = held.tile([P, N], F32, name="s1_all")
+        s0_cols = held.tile([P, RB, NPERM], F32, name="s0_cols")
+        rp_rows = [held.tile([P, NPERM, C], BF16, name=f"rp_rows{cb}") for cb in range(CB)]
+        v = [held.tile([P, H], BF16, name=f"v{cb}") for cb in range(CB)]
+
+        def make_v(cb):
+            rows = slice(cb * P, (cb + 1) * P)
+            logits = loads.tile([P, S], F32, name="logits")
+            nc.sync.dma_start(logits[:], sparse_mask[rows, :])
+            w = loads.tile([P, S], F32, name="w")
+            nc.sync.dma_start(w[:], weight[rows, :])
+            if cb == 0:
+                nc.sync.dma_start(s1_all[:], s1[0, :].partition_broadcast(P))
+                nc.sync.dma_start(s0_cols[:], s0.rearrange("(b p) q -> p b q", p=P))
+            nc.sync.dma_start(rp_rows[cb][:], rp[:, rows, :].rearrange("q p r -> p q r"))
+
+            sig = work.tile([P, S], F32, name="sig")
+            nc.scalar.activation(sig[:], logits[:], ACT.Sigmoid)
+            gate = work.tile([P, S], F32, name="gate")
+            nc.scalar.activation(gate[:], sig[:], ACT.Relu, bias=-0.1, scale=1.2)
+            sw = work.tile([P, S], F32, name="sw")
+            nc.vector.scalar_tensor_tensor(sw[:], gate[:], 1.0, w[:], ALU.min, ALU.mult)
+
+            prod = work.tile([P, N], F32, name="prod")
+            for j in range(0, N, GATHER):
+                nc.vector.tensor_tensor(
+                    prod[:, j : j + GATHER],
+                    sw[:].indirect(offsets[:, j // 16 : (j + GATHER) // 16]),
+                    s1_all[:, j : j + GATHER],
+                    ALU.mult,
+                )
+            pair = work.tile([P, 2 * H], F32, name="pair")
+            nc.gpsimd.tensor_tensor(pair[:], prod[:, : 2 * H], prod[:, 2 * H :], ALU.add)
+            nc.gpsimd.tensor_tensor(v[cb][:], pair[:, :H], pair[:, H:], ALU.add)
+
+        def permute(acc, rb, p, cb):
+            nc.tensor.matmul(
+                acc[:],
+                rp_rows[cb][:, p, rb * P : (rb + 1) * P],
+                v[cb][:],
+                start=(cb == 0),
+                stop=(cb == CB - 1),
+            )
+
+        def finish(accs, rb):
+            total = results.tile([P, H], F32, name="total")
+            nc.scalar.activation(total[:], accs[0][:], ACT.Copy, scale=s0_cols[:, rb, 0:1])
+            for p in range(1, NPERM):
+                nc.vector.scalar_tensor_tensor(
+                    total[:], accs[p][:], s0_cols[:, rb, p : p + 1], total[:], ALU.mult, ALU.add
+                )
+            nc.sync.dma_start(out[rb * P : (rb + 1) * P, :], total[:])
+
+        first = [[psum.tile([P, H], F32, name="acc") for p in range(NPERM)] for rb in range(FIRST_RB)]
+        for cb in range(CB):
+            make_v(cb)
+            for rb in range(FIRST_RB):
+                for p in range(NPERM):
+                    permute(first[rb][p], rb, p, cb)
+        for rb in range(FIRST_RB):
+            finish(first[rb], rb)
+
+        for rb in range(FIRST_RB, RB):
+            accs = [psum.tile([P, H], F32, name="acc") for p in range(NPERM)]
+            for p in range(NPERM):
+                for cb in range(CB):
+                    permute(accs[p], rb, p, cb)
+            finish(accs, rb)

@@ -16,7 +16,9 @@ N = K * H
 CB = C // P
 RB = C // P
 GATHER = S
-FIRST_RB = 8 // NPERM
+BANKS = 8
+PAIR = 2
+WAVE_RB = BANKS * PAIR // NPERM
 
 FLOPS = 2 * NPERM * C * C * H
 
@@ -63,40 +65,47 @@ def tile_permutatedsoftsparse_b_kernel(tc, weight, sparse_mask, s1, s0, rp, offs
                     s1_all[:, j : j + GATHER],
                     ALU.mult,
                 )
-            pair = work.tile([P, 2 * H], F32, name="pair")
-            nc.gpsimd.tensor_tensor(pair[:], prod[:, : 2 * H], prod[:, 2 * H :], ALU.add)
-            nc.gpsimd.tensor_tensor(v[cb][:], pair[:, :H], pair[:, H:], ALU.add)
+            two_sums = work.tile([P, 2 * H], F32, name="two_sums")
+            nc.gpsimd.tensor_tensor(two_sums[:], prod[:, : 2 * H], prod[:, 2 * H :], ALU.add)
+            nc.gpsimd.tensor_tensor(v[cb][:], two_sums[:, :H], two_sums[:, H:], ALU.add)
 
-        def permute(acc, rb, p, cb):
-            nc.tensor.matmul(
-                acc[:],
-                rp_rows[cb][:, p, rb * P : (rb + 1) * P],
-                v[cb][:],
-                start=(cb == 0),
-                stop=(cb == CB - 1),
-            )
+        def open_banks():
+            return [psum.tile([P, PAIR, H], BF16, name="bank") for b in range(NPERM // PAIR)]
 
-        def finish(accs, rb):
+        def permute(banks, rb, cb):
+            for p in range(NPERM):
+                nc.tensor.matmul(
+                    banks[p // PAIR][:, p % PAIR, :],
+                    rp_rows[cb][:, p, rb * P : (rb + 1) * P],
+                    v[cb][:],
+                    start=(cb == 0 and p % PAIR == 0),
+                    stop=(cb == CB - 1 and p % PAIR == PAIR - 1),
+                )
+
+        def finish(banks, rb):
             total = results.tile([P, H], F32, name="total")
-            nc.scalar.activation(total[:], accs[0][:], ACT.Copy, scale=s0_cols[:, rb, 0:1])
+            nc.scalar.activation(total[:], banks[0][:, 0, :], ACT.Copy, scale=s0_cols[:, rb, 0:1])
             for p in range(1, NPERM):
                 nc.vector.scalar_tensor_tensor(
-                    total[:], accs[p][:], s0_cols[:, rb, p : p + 1], total[:], ALU.mult, ALU.add
+                    total[:],
+                    banks[p // PAIR][:, p % PAIR, :],
+                    s0_cols[:, rb, p : p + 1],
+                    total[:],
+                    ALU.mult,
+                    ALU.add,
                 )
             nc.sync.dma_start(out[rb * P : (rb + 1) * P, :], total[:])
 
-        first = [[psum.tile([P, H], F32, name="acc") for p in range(NPERM)] for rb in range(FIRST_RB)]
+        first = [open_banks() for rb in range(WAVE_RB)]
         for cb in range(CB):
             make_v(cb)
-            for rb in range(FIRST_RB):
-                for p in range(NPERM):
-                    permute(first[rb][p], rb, p, cb)
-        for rb in range(FIRST_RB):
+            for rb in range(WAVE_RB):
+                permute(first[rb], rb, cb)
+        for rb in range(WAVE_RB):
             finish(first[rb], rb)
 
-        for rb in range(FIRST_RB, RB):
-            accs = [psum.tile([P, H], F32, name="acc") for p in range(NPERM)]
-            for p in range(NPERM):
-                for cb in range(CB):
-                    permute(accs[p], rb, p, cb)
-            finish(accs, rb)
+        for rb in range(WAVE_RB, RB):
+            banks = open_banks()
+            for cb in range(CB):
+                permute(banks, rb, cb)
+            finish(banks, rb)

@@ -15,10 +15,11 @@ NPERM = 4
 N = K * H
 CB = C // P
 RB = C // P
-GATHER = S
 BANKS = 8
-PAIR = 2
-WAVE_RB = BANKS * PAIR // NPERM
+BANK_BF16 = 1024
+PART = BANK_BF16 // NPERM
+PASSES = H // PART
+AHEAD = 2
 
 FLOPS = 2 * NPERM * C * C * H
 
@@ -29,83 +30,92 @@ def tile_permutatedsoftsparse_b_kernel(tc, weight, sparse_mask, s1, s0, rp, offs
         tc.tile_pool(name="held", bufs=1) as held,
         tc.tile_pool(name="loads", bufs=3) as loads,
         tc.tile_pool(name="work", bufs=2) as work,
-        tc.tile_pool(name="results", bufs=2) as results,
-        tc.psum_pool(name="psum", bufs=8) as psum,
+        tc.tile_pool(name="results", bufs=RB) as results,
+        tc.psum_pool(name="psum", bufs=BANKS) as psum,
     ):
         offsets = held.tile([P, N // 16], U16, name="offsets")
         nc.sync.dma_start(offsets[:], offs)
         s1_all = held.tile([P, N], F32, name="s1_all")
         s0_cols = held.tile([P, RB, NPERM], F32, name="s0_cols")
         rp_rows = [held.tile([P, NPERM, C], BF16, name=f"rp_rows{cb}") for cb in range(CB)]
-        v = [held.tile([P, H], BF16, name=f"v{cb}") for cb in range(CB)]
+        sw = [held.tile([P, S], F32, name=f"sw{cb}") for cb in range(CB)]
+        v = [[held.tile([P, PART], BF16, name=f"v{t}_{cb}") for cb in range(CB)] for t in range(PASSES)]
 
-        def make_v(cb):
+        def load_rows(cb):
             rows = slice(cb * P, (cb + 1) * P)
             logits = loads.tile([P, S], F32, name="logits")
             nc.sync.dma_start(logits[:], sparse_mask[rows, :])
             w = loads.tile([P, S], F32, name="w")
             nc.sync.dma_start(w[:], weight[rows, :])
-            if cb == 0:
-                nc.sync.dma_start(s1_all[:], s1[0, :].partition_broadcast(P))
-                nc.sync.dma_start(s0_cols[:], s0.rearrange("(b p) q -> p b q", p=P))
-            nc.sync.dma_start(rp_rows[cb][:], rp[:, rows, :].rearrange("q p r -> p q r"))
+            return logits, w
 
+        def make_sw(cb, logits, w):
             sig = work.tile([P, S], F32, name="sig")
             nc.scalar.activation(sig[:], logits[:], ACT.Sigmoid)
             gate = work.tile([P, S], F32, name="gate")
             nc.scalar.activation(gate[:], sig[:], ACT.Relu, bias=-0.1, scale=1.2)
-            sw = work.tile([P, S], F32, name="sw")
-            nc.vector.scalar_tensor_tensor(sw[:], gate[:], 1.0, w[:], ALU.min, ALU.mult)
+            nc.vector.scalar_tensor_tensor(sw[cb][:], gate[:], 1.0, w[:], ALU.min, ALU.mult)
 
-            prod = work.tile([P, N], F32, name="prod")
-            for j in range(0, N, GATHER):
+        def make_v(cb, t):
+            prod = work.tile([P, K, PART], F32, name="prod")
+            for k in range(K):
+                j = k * H + t * PART
                 nc.vector.tensor_tensor(
-                    prod[:, j : j + GATHER],
-                    sw[:].indirect(offsets[:, j // 16 : (j + GATHER) // 16]),
-                    s1_all[:, j : j + GATHER],
+                    prod[:, k, :],
+                    sw[cb][:].indirect(offsets[:, j // 16 : (j + PART) // 16]),
+                    s1_all[:, j : j + PART],
                     ALU.mult,
                 )
-            two_sums = work.tile([P, 2 * H], F32, name="two_sums")
-            nc.gpsimd.tensor_tensor(two_sums[:], prod[:, : 2 * H], prod[:, 2 * H :], ALU.add)
-            nc.gpsimd.tensor_tensor(v[cb][:], two_sums[:, :H], two_sums[:, H:], ALU.add)
+            two_sums = work.tile([P, 2, PART], F32, name="two_sums")
+            nc.gpsimd.tensor_tensor(two_sums[:], prod[:, 0:2, :], prod[:, 2:4, :], ALU.add)
+            nc.gpsimd.tensor_tensor(v[t][cb][:], two_sums[:, 0, :], two_sums[:, 1, :], ALU.add)
 
-        def open_banks():
-            return [psum.tile([P, PAIR, H], BF16, name="bank") for b in range(NPERM // PAIR)]
-
-        def permute(banks, rb, cb):
+        def permute(bank, rb, cb, t):
             for p in range(NPERM):
                 nc.tensor.matmul(
-                    banks[p // PAIR][:, p % PAIR, :],
+                    bank[:, p, :],
                     rp_rows[cb][:, p, rb * P : (rb + 1) * P],
-                    v[cb][:],
-                    start=(cb == 0 and p % PAIR == 0),
-                    stop=(cb == CB - 1 and p % PAIR == PAIR - 1),
+                    v[t][cb][:],
+                    start=(cb == 0 and p == 0),
+                    stop=(cb == CB - 1 and p == NPERM - 1),
                 )
 
-        def finish(banks, rb):
-            total = results.tile([P, H], F32, name="total")
-            nc.scalar.activation(total[:], banks[0][:, 0, :], ACT.Copy, scale=s0_cols[:, rb, 0:1])
-            for p in range(1, NPERM):
+        def finish(bank, rb, t):
+            sums = results.tile([P, 2, PART], F32, name="sums")
+            for i in range(2):
+                nc.scalar.activation(sums[:, i, :], bank[:, i, :], ACT.Copy, scale=s0_cols[:, rb, i : i + 1])
+            for i in range(2):
                 nc.vector.scalar_tensor_tensor(
-                    total[:],
-                    banks[p // PAIR][:, p % PAIR, :],
-                    s0_cols[:, rb, p : p + 1],
-                    total[:],
-                    ALU.mult,
-                    ALU.add,
+                    sums[:, i, :], bank[:, 2 + i, :], s0_cols[:, rb, 2 + i : 3 + i], sums[:, i, :], ALU.mult, ALU.add
                 )
-            nc.sync.dma_start(out[rb * P : (rb + 1) * P, :], total[:])
+            total = results.tile([P, PART], F32, name="total")
+            nc.gpsimd.tensor_tensor(total[:], sums[:, 0, :], sums[:, 1, :], ALU.add)
+            nc.sync.dma_start(out[rb * P : (rb + 1) * P, t * PART : (t + 1) * PART], total[:])
 
-        first = [open_banks() for rb in range(WAVE_RB)]
+        banks = [psum.tile([P, NPERM, PART], BF16, name="bank") for rb in range(RB)]
+        fetched = load_rows(0)
+        nc.sync.dma_start(s1_all[:], s1[0, :].partition_broadcast(P))
         for cb in range(CB):
-            make_v(cb)
-            for rb in range(WAVE_RB):
-                permute(first[rb], rb, cb)
-        for rb in range(WAVE_RB):
-            finish(first[rb], rb)
+            logits, w = fetched
+            if cb + 1 < CB:
+                fetched = load_rows(cb + 1)
+            nc.sync.dma_start(rp_rows[cb][:], rp[:, cb * P : (cb + 1) * P, :].rearrange("q p r -> p q r"))
+            if cb == CB // 2:
+                nc.sync.dma_start(s0_cols[:], s0.rearrange("(b p) q -> p b q", p=P))
+            make_sw(cb, logits, w)
+            make_v(cb, 0)
+            for rb in range(RB):
+                permute(banks[rb], rb, cb, 0)
 
-        for rb in range(WAVE_RB, RB):
-            banks = open_banks()
-            for cb in range(CB):
-                permute(banks, rb, cb)
-            finish(banks, rb)
+        for cb in range(AHEAD):
+            make_v(cb, 1)
+        for rb in range(RB):
+            finish(banks[rb], rb, 0)
+        banks = [psum.tile([P, NPERM, PART], BF16, name="bank") for rb in range(RB)]
+        for cb in range(CB):
+            if cb >= AHEAD:
+                make_v(cb, 1)
+            for rb in range(RB):
+                permute(banks[rb], rb, cb, 1)
+        for rb in range(RB):
+            finish(banks[rb], rb, 1)

@@ -19,7 +19,6 @@ BANKS = 8
 BANK_BF16 = 1024
 PART = BANK_BF16 // NPERM
 PASSES = H // PART
-AHEAD = 2
 
 FLOPS = 2 * NPERM * C * C * H
 
@@ -107,15 +106,16 @@ def tile_permutatedsoftsparse_b_kernel(tc, weight, sparse_mask, s1, s0, rp, offs
             for rb in range(RB):
                 permute(banks[rb], rb, cb, 0)
 
-        for cb in range(AHEAD):
-            make_v(cb, 1)
+        parked = [results.tile([P, NPERM, PART], BF16, name="parked") for rb in range(RB)]
         for rb in range(RB):
-            finish(banks[rb], rb, 0)
+            nc.scalar.copy(parked[rb][:], banks[rb][:])
+
         banks = [psum.tile([P, NPERM, PART], BF16, name="bank") for rb in range(RB)]
         for cb in range(CB):
-            if cb >= AHEAD:
-                make_v(cb, 1)
+            make_v(cb, 1)
             for rb in range(RB):
                 permute(banks[rb], rb, cb, 1)
+        for rb in range(RB):
+            finish(parked[rb], rb, 0)
         for rb in range(RB):
             finish(banks[rb], rb, 1)

@@ -66,8 +66,8 @@ def tile_permutatedsoftsparse_b_kernel(tc, weight, sparse_mask, s1, s0, rp, offs
                     ALU.mult,
                 )
             two_sums = work.tile([P, 2, PART], F32, name="two_sums")
-            nc.gpsimd.tensor_tensor(two_sums[:], prod[:, 0:2, :], prod[:, 2:4, :], ALU.add)
-            nc.gpsimd.tensor_tensor(v[t][cb][:], two_sums[:, 0, :], two_sums[:, 1, :], ALU.add)
+            nc.vector.tensor_tensor(two_sums[:], prod[:, 0:2, :], prod[:, 2:4, :], ALU.add)
+            nc.vector.tensor_tensor(v[t][cb][:], two_sums[:, 0, :], two_sums[:, 1, :], ALU.add)
 
         def permute(bank, rb, cb, t):
             for p in range(NPERM):
@@ -88,7 +88,7 @@ def tile_permutatedsoftsparse_b_kernel(tc, weight, sparse_mask, s1, s0, rp, offs
                     sums[:, i, :], bank[:, 2 + i, :], s0_cols[:, rb, 2 + i : 3 + i], sums[:, i, :], ALU.mult, ALU.add
                 )
             total = results.tile([P, PART], F32, name="total")
-            nc.gpsimd.tensor_tensor(total[:], sums[:, 0, :], sums[:, 1, :], ALU.add)
+            nc.vector.tensor_tensor(total[:], sums[:, 0, :], sums[:, 1, :], ALU.add)
             nc.sync.dma_start(out[rb * P : (rb + 1) * P, t * PART : (t + 1) * PART], total[:])
 
         banks = [psum.tile([P, NPERM, PART], BF16, name="bank") for rb in range(RB)]

@@ -19,6 +19,7 @@ BANKS = 8
 BANK_BF16 = 1024
 PART = BANK_BF16 // NPERM
 PASSES = H // PART
+LAST = 2
 
 FLOPS = 2 * NPERM * C * C * H
 
@@ -48,14 +49,15 @@ def tile_permutatedsoftsparse_b_kernel(tc, weight, sparse_mask, s1, s0, rp, offs
             nc.sync.dma_start(w[:], weight[rows, :])
             return logits, w
 
-        def make_sw(cb, logits, w):
+        def make_sw(cb, rows):
+            logits, w = rows
             sig = work.tile([P, S], F32, name="sig")
             nc.scalar.activation(sig[:], logits[:], ACT.Sigmoid)
             gate = work.tile([P, S], F32, name="gate")
             nc.scalar.activation(gate[:], sig[:], ACT.Relu, bias=-0.1, scale=1.2)
             nc.vector.scalar_tensor_tensor(sw[cb][:], gate[:], 1.0, w[:], ALU.min, ALU.mult)
 
-        def make_v(cb, t):
+        def look_up(cb, t):
             prod = work.tile([P, K, PART], F32, name="prod")
             for k in range(K):
                 j = k * H + t * PART
@@ -65,9 +67,12 @@ def tile_permutatedsoftsparse_b_kernel(tc, weight, sparse_mask, s1, s0, rp, offs
                     s1_all[:, j : j + PART],
                     ALU.mult,
                 )
-            two_sums = work.tile([P, 2, PART], F32, name="two_sums")
-            nc.vector.tensor_tensor(two_sums[:], prod[:, 0:2, :], prod[:, 2:4, :], ALU.add)
-            nc.vector.tensor_tensor(v[t][cb][:], two_sums[:, 0, :], two_sums[:, 1, :], ALU.add)
+                if k >= 2:
+                    nc.vector.tensor_tensor(prod[:, k - 1, :], prod[:, k - 1, :], prod[:, k - 2, :], ALU.add)
+            return prod
+
+        def sum_over_k(prod, cb, t):
+            nc.vector.tensor_tensor(v[t][cb][:], prod[:, K - 1, :], prod[:, K - 2, :], ALU.add)
 
         def permute(bank, rb, cb, t):
             for p in range(NPERM):
@@ -92,17 +97,20 @@ def tile_permutatedsoftsparse_b_kernel(tc, weight, sparse_mask, s1, s0, rp, offs
             nc.sync.dma_start(out[rb * P : (rb + 1) * P, t * PART : (t + 1) * PART], total[:])
 
         banks = [psum.tile([P, NPERM, PART], BF16, name="bank") for rb in range(RB)]
-        fetched = load_rows(0)
+        fetched = [load_rows(0)]
         nc.sync.dma_start(s1_all[:], s1[0, :].partition_broadcast(P))
+        fetched.append(load_rows(1))
+        make_sw(0, fetched[0])
         for cb in range(CB):
-            logits, w = fetched
-            if cb + 1 < CB:
-                fetched = load_rows(cb + 1)
             nc.sync.dma_start(rp_rows[cb][:], rp[:, cb * P : (cb + 1) * P, :].rearrange("q p r -> p q r"))
+            if cb + 2 < CB:
+                fetched.append(load_rows(cb + 2))
             if cb == CB // 2:
                 nc.sync.dma_start(s0_cols[:], s0.rearrange("(b p) q -> p b q", p=P))
-            make_sw(cb, logits, w)
-            make_v(cb, 0)
+            prod = look_up(cb, 0)
+            if cb + 1 < CB:
+                make_sw(cb + 1, fetched[cb + 1])
+            sum_over_k(prod, cb, 0)
             for rb in range(RB):
                 permute(banks[rb], rb, cb, 0)
 
@@ -112,10 +120,13 @@ def tile_permutatedsoftsparse_b_kernel(tc, weight, sparse_mask, s1, s0, rp, offs
 
         banks = [psum.tile([P, NPERM, PART], BF16, name="bank") for rb in range(RB)]
         for cb in range(CB):
-            make_v(cb, 1)
-            for rb in range(RB):
-                permute(banks[rb], rb, cb, 1)
+            sum_over_k(look_up(cb, 1), cb, 1)
+            if cb < CB - LAST:
+                for rb in range(RB):
+                    permute(banks[rb], rb, cb, 1)
         for rb in range(RB):
             finish(parked[rb], rb, 0)
         for rb in range(RB):
+            for cb in range(CB - LAST, CB):
+                permute(banks[rb], rb, cb, 1)
             finish(banks[rb], rb, 1)

@@ -20,6 +20,7 @@ BANK_BF16 = 1024
 PART = BANK_BF16 // NPERM
 PASSES = H // PART
 LAST = 2
+AHEAD = 2
 
 FLOPS = 2 * NPERM * C * C * H
 
@@ -28,8 +29,7 @@ def tile_permutatedsoftsparse_b_kernel(tc, weight, sparse_mask, s1, s0, rp, offs
     nc = tc.nc
     with (
         tc.tile_pool(name="held", bufs=1) as held,
-        tc.tile_pool(name="loads", bufs=3) as loads,
-        tc.tile_pool(name="work", bufs=2) as work,
+        tc.tile_pool(name="work", bufs=AHEAD + 1) as work,
         tc.tile_pool(name="results", bufs=RB) as results,
         tc.psum_pool(name="psum", bufs=BANKS) as psum,
     ):
@@ -38,26 +38,23 @@ def tile_permutatedsoftsparse_b_kernel(tc, weight, sparse_mask, s1, s0, rp, offs
         s1_all = held.tile([P, N], F32, name="s1_all")
         s0_cols = held.tile([P, RB, NPERM], F32, name="s0_cols")
         rp_rows = [held.tile([P, NPERM, C], BF16, name=f"rp_rows{cb}") for cb in range(CB)]
+        logits = [held.tile([P, S], F32, name=f"logits{cb}") for cb in range(CB)]
         sw = [held.tile([P, S], F32, name=f"sw{cb}") for cb in range(CB)]
         v = [[held.tile([P, PART], BF16, name=f"v{t}_{cb}") for cb in range(CB)] for t in range(PASSES)]
 
         def load_rows(cb):
             rows = slice(cb * P, (cb + 1) * P)
-            logits = loads.tile([P, S], F32, name="logits")
-            nc.sync.dma_start(logits[:], sparse_mask[rows, :])
-            w = loads.tile([P, S], F32, name="w")
-            nc.sync.dma_start(w[:], weight[rows, :])
-            return logits, w
+            nc.sync.dma_start(logits[cb][:], sparse_mask[rows, :])
+            nc.sync.dma_start(sw[cb][:], weight[rows, :])
 
-        def make_sw(cb, rows):
-            logits, w = rows
+        def make_sw(cb):
             sig = work.tile([P, S], F32, name="sig")
-            nc.scalar.activation(sig[:], logits[:], ACT.Sigmoid)
+            nc.scalar.activation(sig[:], logits[cb][:], ACT.Sigmoid)
             gate = work.tile([P, S], F32, name="gate")
             nc.scalar.activation(gate[:], sig[:], ACT.Relu, bias=-0.1, scale=1.2)
-            nc.vector.scalar_tensor_tensor(sw[cb][:], gate[:], 1.0, w[:], ALU.min, ALU.mult)
+            nc.vector.scalar_tensor_tensor(sw[cb][:], gate[:], 1.0, sw[cb][:], ALU.min, ALU.mult)
 
-        def look_up(cb, t):
+        def make_v(cb, t):
             prod = work.tile([P, K, PART], F32, name="prod")
             for k in range(K):
                 j = k * H + t * PART
@@ -69,9 +66,6 @@ def tile_permutatedsoftsparse_b_kernel(tc, weight, sparse_mask, s1, s0, rp, offs
                 )
                 if k >= 2:
                     nc.vector.tensor_tensor(prod[:, k - 1, :], prod[:, k - 1, :], prod[:, k - 2, :], ALU.add)
-            return prod
-
-        def sum_over_k(prod, cb, t):
             nc.vector.tensor_tensor(v[t][cb][:], prod[:, K - 1, :], prod[:, K - 2, :], ALU.add)
 
         def permute(bank, rb, cb, t):
@@ -84,49 +78,50 @@ def tile_permutatedsoftsparse_b_kernel(tc, weight, sparse_mask, s1, s0, rp, offs
                     stop=(cb == CB - 1 and p == NPERM - 1),
                 )
 
-        def finish(bank, rb, t):
+        def read_out(acc, rb, t):
             sums = results.tile([P, 2, PART], F32, name="sums")
             for i in range(2):
-                nc.scalar.activation(sums[:, i, :], bank[:, i, :], ACT.Copy, scale=s0_cols[:, rb, i : i + 1])
+                nc.scalar.activation(sums[:, i, :], acc[:, i, :], ACT.Copy, scale=s0_cols[:, rb, i : i + 1])
             for i in range(2):
+                p = i + 2
                 nc.vector.scalar_tensor_tensor(
-                    sums[:, i, :], bank[:, 2 + i, :], s0_cols[:, rb, 2 + i : 3 + i], sums[:, i, :], ALU.mult, ALU.add
+                    sums[:, i, :], acc[:, p, :], s0_cols[:, rb, p : p + 1], sums[:, i, :], ALU.mult, ALU.add
                 )
             total = results.tile([P, PART], F32, name="total")
             nc.vector.tensor_tensor(total[:], sums[:, 0, :], sums[:, 1, :], ALU.add)
             nc.sync.dma_start(out[rb * P : (rb + 1) * P, t * PART : (t + 1) * PART], total[:])
 
-        banks = [psum.tile([P, NPERM, PART], BF16, name="bank") for rb in range(RB)]
-        fetched = [load_rows(0)]
+        def open_banks():
+            return [psum.tile([P, NPERM, PART], BF16, name="bank") for rb in range(RB)]
+
+        first_banks = open_banks()
+        load_rows(0)
         nc.sync.dma_start(s1_all[:], s1[0, :].partition_broadcast(P))
-        fetched.append(load_rows(1))
-        make_sw(0, fetched[0])
+        for cb in range(1, AHEAD):
+            load_rows(cb)
         for cb in range(CB):
+            if cb + AHEAD < CB:
+                load_rows(cb + AHEAD)
             nc.sync.dma_start(rp_rows[cb][:], rp[:, cb * P : (cb + 1) * P, :].rearrange("q p r -> p q r"))
-            if cb + 2 < CB:
-                fetched.append(load_rows(cb + 2))
-            if cb == CB // 2:
-                nc.sync.dma_start(s0_cols[:], s0.rearrange("(b p) q -> p b q", p=P))
-            prod = look_up(cb, 0)
-            if cb + 1 < CB:
-                make_sw(cb + 1, fetched[cb + 1])
-            sum_over_k(prod, cb, 0)
+            make_sw(cb)
+            make_v(cb, 0)
             for rb in range(RB):
-                permute(banks[rb], rb, cb, 0)
+                permute(first_banks[rb], rb, cb, 0)
+        nc.sync.dma_start(s0_cols[:], s0.rearrange("(b p) q -> p b q", p=P))
 
         parked = [results.tile([P, NPERM, PART], BF16, name="parked") for rb in range(RB)]
         for rb in range(RB):
-            nc.scalar.copy(parked[rb][:], banks[rb][:])
+            nc.scalar.copy(parked[rb][:], first_banks[rb][:])
 
-        banks = [psum.tile([P, NPERM, PART], BF16, name="bank") for rb in range(RB)]
+        second_banks = open_banks()
         for cb in range(CB):
-            sum_over_k(look_up(cb, 1), cb, 1)
+            make_v(cb, 1)
             if cb < CB - LAST:
                 for rb in range(RB):
-                    permute(banks[rb], rb, cb, 1)
+                    permute(second_banks[rb], rb, cb, 1)
         for rb in range(RB):
-            finish(parked[rb], rb, 0)
+            read_out(parked[rb], rb, 0)
         for rb in range(RB):
             for cb in range(CB - LAST, CB):
-                permute(banks[rb], rb, cb, 1)
-            finish(banks[rb], rb, 1)
+                permute(second_banks[rb], rb, cb, 1)
+            read_out(second_banks[rb], rb, 1)

@@ -21,6 +21,7 @@ PART = BANK_BF16 // NPERM
 PASSES = H // PART
 LAST = 2
 AHEAD = 2
+FIRST_PIECES = 4
 
 FLOPS = 2 * NPERM * C * C * H
 
@@ -42,17 +43,23 @@ def tile_permutatedsoftsparse_b_kernel(tc, weight, sparse_mask, s1, s0, rp, offs
         sw = [held.tile([P, S], F32, name=f"sw{cb}") for cb in range(CB)]
         v = [[held.tile([P, PART], BF16, name=f"v{t}_{cb}") for cb in range(CB)] for t in range(PASSES)]
 
+        def pieces_of(cb):
+            pieces = FIRST_PIECES if cb == 0 else 1
+            return [slice(i * S // pieces, (i + 1) * S // pieces) for i in range(pieces)]
+
         def load_rows(cb):
             rows = slice(cb * P, (cb + 1) * P)
-            nc.sync.dma_start(logits[cb][:], sparse_mask[rows, :])
-            nc.sync.dma_start(sw[cb][:], weight[rows, :])
+            for cols in pieces_of(cb):
+                nc.sync.dma_start(logits[cb][:, cols], sparse_mask[rows, cols])
+                nc.sync.dma_start(sw[cb][:, cols], weight[rows, cols])
 
         def make_sw(cb):
             sig = work.tile([P, S], F32, name="sig")
-            nc.scalar.activation(sig[:], logits[cb][:], ACT.Sigmoid)
             gate = work.tile([P, S], F32, name="gate")
-            nc.scalar.activation(gate[:], sig[:], ACT.Relu, bias=-0.1, scale=1.2)
-            nc.vector.scalar_tensor_tensor(sw[cb][:], gate[:], 1.0, sw[cb][:], ALU.min, ALU.mult)
+            for cols in pieces_of(cb):
+                nc.scalar.activation(sig[:, cols], logits[cb][:, cols], ACT.Sigmoid)
+                nc.scalar.activation(gate[:, cols], sig[:, cols], ACT.Relu, bias=-0.1, scale=1.2)
+                nc.vector.scalar_tensor_tensor(sw[cb][:, cols], gate[:, cols], 1.0, sw[cb][:, cols], ALU.min, ALU.mult)
 
         def make_v(cb, t):
             prod = work.tile([P, K, PART], F32, name="prod")

@@ -19,7 +19,7 @@ BANKS = 8
 BANK_BF16 = 1024
 PART = BANK_BF16 // NPERM
 PASSES = H // PART
-LAST = 2
+LAST = 3
 AHEAD = 2
 FIRST_PIECES = 4
 

@@ -19,9 +19,12 @@ BANKS = 8
 BANK_BF16 = 1024
 PART = BANK_BF16 // NPERM
 PASSES = H // PART
+F32_BYTES = 4
 LAST = 3
 AHEAD = 2
-FIRST_PIECES = 4
+EARLY = 2
+PIECES = 4
+HALF_FIRST = 2
 
 FLOPS = 2 * NPERM * C * C * H
 
@@ -30,21 +33,31 @@ def tile_permutatedsoftsparse_b_kernel(tc, weight, sparse_mask, s1, s0, rp, offs
     nc = tc.nc
     with (
         tc.tile_pool(name="held", bufs=1) as held,
+        tc.tile_pool(name="rows_in", bufs=1) as rows_in,
         tc.tile_pool(name="work", bufs=AHEAD + 1) as work,
         tc.tile_pool(name="results", bufs=RB) as results,
         tc.psum_pool(name="psum", bufs=BANKS) as psum,
     ):
+        def paced(cb):
+            return 0 < cb < CB - 1
+
+        def v_tile(t, cb):
+            if t == 0 and paced(cb):
+                return rows_in.tile([P, PART], BF16, name=f"v{t}_{cb}", offset=(cb + 1) * S * F32_BYTES)
+            return held.tile([P, PART], BF16, name=f"v{t}_{cb}")
+
         offsets = held.tile([P, N // 16], U16, name="offsets")
         nc.sync.dma_start(offsets[:], offs)
         s1_all = held.tile([P, N], F32, name="s1_all")
         s0_cols = held.tile([P, RB, NPERM], F32, name="s0_cols")
         rp_rows = [held.tile([P, NPERM, C], BF16, name=f"rp_rows{cb}") for cb in range(CB)]
-        logits = [held.tile([P, S], F32, name=f"logits{cb}") for cb in range(CB)]
+        logits = [rows_in.tile([P, S], F32, name=f"logits{cb}", offset=cb * S * F32_BYTES) for cb in range(CB)]
         sw = [held.tile([P, S], F32, name=f"sw{cb}") for cb in range(CB)]
-        v = [[held.tile([P, PART], BF16, name=f"v{t}_{cb}") for cb in range(CB)] for t in range(PASSES)]
+        prod = held.tile([P, K, PART], F32, name="prod")
+        v = [[v_tile(t, cb) for cb in range(CB)] for t in range(PASSES)]
 
         def pieces_of(cb):
-            pieces = FIRST_PIECES if cb == 0 else 1
+            pieces = PIECES if cb < EARLY else 1
             return [slice(i * S // pieces, (i + 1) * S // pieces) for i in range(pieces)]
 
         def load_rows(cb):
@@ -54,15 +67,13 @@ def tile_permutatedsoftsparse_b_kernel(tc, weight, sparse_mask, s1, s0, rp, offs
                 nc.sync.dma_start(sw[cb][:, cols], weight[rows, cols])
 
         def make_sw(cb):
-            sig = work.tile([P, S], F32, name="sig")
             gate = work.tile([P, S], F32, name="gate")
             for cols in pieces_of(cb):
-                nc.scalar.activation(sig[:, cols], logits[cb][:, cols], ACT.Sigmoid)
-                nc.scalar.activation(gate[:, cols], sig[:, cols], ACT.Relu, bias=-0.1, scale=1.2)
+                nc.scalar.activation(logits[cb][:, cols], logits[cb][:, cols], ACT.Sigmoid)
+                nc.scalar.activation(gate[:, cols], logits[cb][:, cols], ACT.Relu, bias=-0.1, scale=1.2)
                 nc.vector.scalar_tensor_tensor(sw[cb][:, cols], gate[:, cols], 1.0, sw[cb][:, cols], ALU.min, ALU.mult)
 
-        def make_v(cb, t):
-            prod = work.tile([P, K, PART], F32, name="prod")
+        def look_up(cb, t, after_first=None):
             for k in range(K):
                 j = k * H + t * PART
                 nc.vector.tensor_tensor(
@@ -71,12 +82,16 @@ def tile_permutatedsoftsparse_b_kernel(tc, weight, sparse_mask, s1, s0, rp, offs
                     s1_all[:, j : j + PART],
                     ALU.mult,
                 )
+                if k == 0 and after_first:
+                    after_first()
                 if k >= 2:
                     nc.vector.tensor_tensor(prod[:, k - 1, :], prod[:, k - 1, :], prod[:, k - 2, :], ALU.add)
+
+        def finish_v(cb, t):
             nc.vector.tensor_tensor(v[t][cb][:], prod[:, K - 1, :], prod[:, K - 2, :], ALU.add)
 
-        def permute(bank, rb, cb, t):
-            for p in range(NPERM):
+        def permute(bank, rb, cb, t, perms=range(NPERM)):
+            for p in perms:
                 nc.tensor.matmul(
                     bank[:, p, :],
                     rp_rows[cb][:, p, rb * P : (rb + 1) * P],
@@ -85,18 +100,35 @@ def tile_permutatedsoftsparse_b_kernel(tc, weight, sparse_mask, s1, s0, rp, offs
                     stop=(cb == CB - 1 and p == NPERM - 1),
                 )
 
-        def read_out(acc, rb, t):
-            sums = results.tile([P, 2, PART], F32, name="sums")
+        def store(total, rb, t):
+            nc.sync.dma_start(out[rb * P : (rb + 1) * P, t * PART : (t + 1) * PART], total[:])
+
+        def clear_bank(bank, rb):
+            terms = results.tile([P, NPERM, PART], F32, name="terms")
+            for p in range(NPERM):
+                nc.scalar.activation(terms[:, p, :], bank[:, p, :], ACT.Copy, scale=s0_cols[:, rb, p : p + 1])
+            return terms
+
+        def add_terms(terms, rb, t):
+            half = NPERM // 2
+            pairs = results.tile([P, half, PART], F32, name="pairs")
+            nc.vector.tensor_tensor(pairs[:], terms[:, :half, :], terms[:, half:, :], ALU.add)
+            total = results.tile([P, PART], F32, name="total")
+            nc.vector.tensor_tensor(total[:], pairs[:, 0, :], pairs[:, 1, :], ALU.add)
+            store(total, rb, t)
+
+        def read_out(bank, rb, t):
+            sums = results.tile([P, NPERM // 2, PART], F32, name="pairs")
             for i in range(2):
-                nc.scalar.activation(sums[:, i, :], acc[:, i, :], ACT.Copy, scale=s0_cols[:, rb, i : i + 1])
+                nc.scalar.activation(sums[:, i, :], bank[:, i, :], ACT.Copy, scale=s0_cols[:, rb, i : i + 1])
             for i in range(2):
                 p = i + 2
                 nc.vector.scalar_tensor_tensor(
-                    sums[:, i, :], acc[:, p, :], s0_cols[:, rb, p : p + 1], sums[:, i, :], ALU.mult, ALU.add
+                    sums[:, i, :], bank[:, p, :], s0_cols[:, rb, p : p + 1], sums[:, i, :], ALU.mult, ALU.add
                 )
             total = results.tile([P, PART], F32, name="total")
             nc.vector.tensor_tensor(total[:], sums[:, 0, :], sums[:, 1, :], ALU.add)
-            nc.sync.dma_start(out[rb * P : (rb + 1) * P, t * PART : (t + 1) * PART], total[:])
+            store(total, rb, t)
 
         def open_banks():
             return [psum.tile([P, NPERM, PART], BF16, name="bank") for rb in range(RB)]
@@ -106,28 +138,46 @@ def tile_permutatedsoftsparse_b_kernel(tc, weight, sparse_mask, s1, s0, rp, offs
         nc.sync.dma_start(s1_all[:], s1[0, :].partition_broadcast(P))
         for cb in range(1, AHEAD):
             load_rows(cb)
+        make_sw(0)
         for cb in range(CB):
             if cb + AHEAD < CB:
                 load_rows(cb + AHEAD)
-            nc.sync.dma_start(rp_rows[cb][:], rp[:, cb * P : (cb + 1) * P, :].rearrange("q p r -> p q r"))
-            make_sw(cb)
-            make_v(cb, 0)
-            for rb in range(RB):
-                permute(first_banks[rb], rb, cb, 0)
+            for p in range(NPERM):
+                nc.sync.dma_start(rp_rows[cb][:, p, :], rp[p, cb * P : (cb + 1) * P, :])
+            look_up(cb, 0)
+            if paced(cb):
+                make_sw(cb + 1)
+                finish_v(cb, 0)
+            else:
+                finish_v(cb, 0)
+                if cb + 1 < CB:
+                    make_sw(cb + 1)
+            if cb < CB - 1:
+                for p in range(NPERM):
+                    for rb in range(RB):
+                        permute(first_banks[rb], rb, cb, 0, [p])
+            else:
+                for rb in range(RB):
+                    permute(first_banks[rb], rb, cb, 0)
         nc.sync.dma_start(s0_cols[:], s0.rearrange("(b p) q -> p b q", p=P))
 
-        parked = [results.tile([P, NPERM, PART], BF16, name="parked") for rb in range(RB)]
-        for rb in range(RB):
-            nc.scalar.copy(parked[rb][:], first_banks[rb][:])
+        terms = [clear_bank(first_banks[rb], rb) for rb in range(RB)]
 
         second_banks = open_banks()
         for cb in range(CB):
-            make_v(cb, 1)
-            if cb < CB - LAST:
+            look_up(cb, 1, lambda: finish_v(cb - 1, 1) if cb > 0 else None)
+        finish_v(CB - 1, 1)
+        for cb in range(CB):
+            if cb == HALF_FIRST - 1:
+                for half in (range(RB // 2), range(RB // 2, RB)):
+                    for early in range(HALF_FIRST):
+                        for rb in half:
+                            permute(second_banks[rb], rb, early, 1)
+            elif HALF_FIRST <= cb < CB - LAST:
                 for rb in range(RB):
                     permute(second_banks[rb], rb, cb, 1)
         for rb in range(RB):
-            read_out(parked[rb], rb, 0)
+            add_terms(terms[rb], rb, 0)
         for rb in range(RB):
             for cb in range(CB - LAST, CB):
                 permute(second_banks[rb], rb, cb, 1)

@@ -66,6 +66,9 @@ def tile_permutatedsoftsparse_b_kernel(tc, weight, sparse_mask, s1, s0, rp, offs
                 nc.sync.dma_start(logits[cb][:, cols], sparse_mask[rows, cols])
                 nc.sync.dma_start(sw[cb][:, cols], weight[rows, cols])
 
+        def load_rp(cb, p):
+            nc.sync.dma_start(rp_rows[cb][:, p, :], rp[p, cb * P : (cb + 1) * P, :])
+
         def make_sw(cb):
             gate = work.tile([P, S], F32, name="gate")
             for cols in pieces_of(cb):
@@ -138,12 +141,13 @@ def tile_permutatedsoftsparse_b_kernel(tc, weight, sparse_mask, s1, s0, rp, offs
         nc.sync.dma_start(s1_all[:], s1[0, :].partition_broadcast(P))
         for cb in range(1, AHEAD):
             load_rows(cb)
+        load_rp(0, 0)
         make_sw(0)
         for cb in range(CB):
             if cb + AHEAD < CB:
                 load_rows(cb + AHEAD)
-            for p in range(NPERM):
-                nc.sync.dma_start(rp_rows[cb][:, p, :], rp[p, cb * P : (cb + 1) * P, :])
+            for p in range(1 if cb == 0 else 0, NPERM):
+                load_rp(cb, p)
             look_up(cb, 0)
             if paced(cb):
                 make_sw(cb + 1)

@@ -20,7 +20,7 @@ BANK_BF16 = 1024
 PART = BANK_BF16 // NPERM
 PASSES = H // PART
 F32_BYTES = 4
-LAST = 3
+LAST = 2
 AHEAD = 2
 EARLY = 2
 PIECES = 4
@@ -112,13 +112,16 @@ def tile_permutatedsoftsparse_b_kernel(tc, weight, sparse_mask, s1, s0, rp, offs
                 nc.scalar.activation(terms[:, p, :], bank[:, p, :], ACT.Copy, scale=s0_cols[:, rb, p : p + 1])
             return terms
 
-        def add_terms(terms, rb, t):
+        def add_pairs(terms):
             half = NPERM // 2
             pairs = results.tile([P, half, PART], F32, name="pairs")
             nc.vector.tensor_tensor(pairs[:], terms[:, :half, :], terms[:, half:, :], ALU.add)
+            return pairs
+
+        def add_pair(pairs):
             total = results.tile([P, PART], F32, name="total")
             nc.vector.tensor_tensor(total[:], pairs[:, 0, :], pairs[:, 1, :], ALU.add)
-            store(total, rb, t)
+            return total
 
         def read_out(bank, rb, t):
             sums = results.tile([P, NPERM // 2, PART], F32, name="pairs")
@@ -129,14 +132,34 @@ def tile_permutatedsoftsparse_b_kernel(tc, weight, sparse_mask, s1, s0, rp, offs
                 nc.vector.scalar_tensor_tensor(
                     sums[:, i, :], bank[:, p, :], s0_cols[:, rb, p : p + 1], sums[:, i, :], ALU.mult, ALU.add
                 )
-            total = results.tile([P, PART], F32, name="total")
-            nc.vector.tensor_tensor(total[:], sums[:, 0, :], sums[:, 1, :], ALU.add)
+            store(add_pair(sums), rb, t)
+
+        def last_output_block():
+            rb, t = RB - 1, PASSES - 1
+            total = None
+            for p in range(NPERM):
+                bank = psum.tile([P, PART], BF16, name="last_bank", tag="bank")
+                for cb in range(CB):
+                    nc.tensor.matmul(
+                        bank[:],
+                        rp_rows[cb][:, p, rb * P : (rb + 1) * P],
+                        v[t][cb][:],
+                        start=(cb == 0),
+                        stop=(cb == CB - 1),
+                    )
+                scale = s0_cols[:, rb, p : p + 1]
+                more = results.tile([P, PART], F32, name="total")
+                if p == 0:
+                    nc.scalar.activation(more[:], bank[:], ACT.Copy, scale=scale)
+                else:
+                    nc.vector.scalar_tensor_tensor(more[:], bank[:], scale, total[:], ALU.mult, ALU.add)
+                total = more
             store(total, rb, t)
 
-        def open_banks():
-            return [psum.tile([P, NPERM, PART], BF16, name="bank") for rb in range(RB)]
+        def open_banks(blocks):
+            return [psum.tile([P, NPERM, PART], BF16, name="bank", tag="bank") for rb in range(blocks)]
 
-        first_banks = open_banks()
+        first_banks = open_banks(RB)
         load_rows(0)
         nc.sync.dma_start(s1_all[:], s1[0, :].partition_broadcast(P))
         for cb in range(1, AHEAD):
@@ -167,22 +190,26 @@ def tile_permutatedsoftsparse_b_kernel(tc, weight, sparse_mask, s1, s0, rp, offs
 
         terms = [clear_bank(first_banks[rb], rb) for rb in range(RB)]
 
-        second_banks = open_banks()
+        second_banks = open_banks(RB - 1)
         for cb in range(CB):
             look_up(cb, 1, lambda: finish_v(cb - 1, 1) if cb > 0 else None)
         finish_v(CB - 1, 1)
         for cb in range(CB):
             if cb == HALF_FIRST - 1:
-                for half in (range(RB // 2), range(RB // 2, RB)):
+                for half in (range(RB // 2), range(RB // 2, RB - 1)):
                     for early in range(HALF_FIRST):
                         for rb in half:
                             permute(second_banks[rb], rb, early, 1)
             elif HALF_FIRST <= cb < CB - LAST:
-                for rb in range(RB):
+                for rb in range(RB - 1):
                     permute(second_banks[rb], rb, cb, 1)
+        pairs = add_pairs(terms[0])
         for rb in range(RB):
-            add_terms(terms[rb], rb, 0)
-        for rb in range(RB):
+            next_pairs = add_pairs(terms[rb + 1]) if rb + 1 < RB else None
+            store(add_pair(pairs), rb, 0)
+            pairs = next_pairs
+        for rb in range(RB - 1):
             for cb in range(CB - LAST, CB):
                 permute(second_banks[rb], rb, cb, 1)
             read_out(second_banks[rb], rb, 1)
+        last_output_block()

@@ -64,6 +64,7 @@ def tile_permutatedsoftsparse_b_kernel(tc, weight, sparse_mask, s1, s0, rp, offs
             rows = slice(cb * P, (cb + 1) * P)
             for cols in pieces_of(cb):
                 nc.sync.dma_start(logits[cb][:, cols], sparse_mask[rows, cols])
+            for cols in pieces_of(cb):
                 nc.sync.dma_start(sw[cb][:, cols], weight[rows, cols])
 
         def load_rp(cb, p):
@@ -73,7 +74,9 @@ def tile_permutatedsoftsparse_b_kernel(tc, weight, sparse_mask, s1, s0, rp, offs
             gate = work.tile([P, S], F32, name="gate")
             for cols in pieces_of(cb):
                 nc.scalar.activation(logits[cb][:, cols], logits[cb][:, cols], ACT.Sigmoid)
+            for cols in pieces_of(cb):
                 nc.scalar.activation(gate[:, cols], logits[cb][:, cols], ACT.Relu, bias=-0.1, scale=1.2)
+            for cols in pieces_of(cb):
                 nc.vector.scalar_tensor_tensor(sw[cb][:, cols], gate[:, cols], 1.0, sw[cb][:, cols], ALU.min, ALU.mult)
 
         def look_up(cb, t, after_first=None):

@@ -23,7 +23,8 @@ F32_BYTES = 4
 LAST = 2
 AHEAD = 2
 EARLY = 2
-PIECES = 4
+EARLY_RUNS = 4
+LATER_RUNS = 2
 HALF_FIRST = 2
 
 FLOPS = 2 * NPERM * C * C * H
@@ -56,27 +57,26 @@ def tile_permutatedsoftsparse_b_kernel(tc, weight, sparse_mask, s1, s0, rp, offs
         prod = held.tile([P, K, PART], F32, name="prod")
         v = [[v_tile(t, cb) for cb in range(CB)] for t in range(PASSES)]
 
-        def pieces_of(cb):
-            pieces = PIECES if cb < EARLY else 1
-            return [slice(i * S // pieces, (i + 1) * S // pieces) for i in range(pieces)]
+        def runs_of(count):
+            return [slice(i * S // count, (i + 1) * S // count) for i in range(count)]
 
         def load_rows(cb):
             rows = slice(cb * P, (cb + 1) * P)
-            for cols in pieces_of(cb):
+            for cols in runs_of(EARLY_RUNS if cb < EARLY else 1):
                 nc.sync.dma_start(logits[cb][:, cols], sparse_mask[rows, cols])
-            for cols in pieces_of(cb):
                 nc.sync.dma_start(sw[cb][:, cols], weight[rows, cols])
 
         def load_rp(cb, p):
             nc.sync.dma_start(rp_rows[cb][:, p, :], rp[p, cb * P : (cb + 1) * P, :])
 
         def make_sw(cb):
+            runs = runs_of(EARLY_RUNS if cb < EARLY else LATER_RUNS)
             gate = work.tile([P, S], F32, name="gate")
-            for cols in pieces_of(cb):
+            for cols in runs:
                 nc.scalar.activation(logits[cb][:, cols], logits[cb][:, cols], ACT.Sigmoid)
-            for cols in pieces_of(cb):
+            for cols in runs:
                 nc.scalar.activation(gate[:, cols], logits[cb][:, cols], ACT.Relu, bias=-0.1, scale=1.2)
-            for cols in pieces_of(cb):
+            for cols in runs:
                 nc.vector.scalar_tensor_tensor(sw[cb][:, cols], gate[:, cols], 1.0, sw[cb][:, cols], ALU.min, ALU.mult)
 
         def look_up(cb, t, after_first=None):

import concourse.mybir as mybir

F32 = mybir.dt.float32
BF16 = mybir.dt.bfloat16
U16 = mybir.dt.uint16
ALU = mybir.AluOpType
ACT = mybir.ActivationFunctionType

P = 128
C = 1024
S = 1024
H = 512
K = 4
NPERM = 4
N = K * H
CB = C // P
RB = C // P
BANKS = 8
BANK_BF16 = 1024
PART = BANK_BF16 // NPERM
PASSES = H // PART
F32_BYTES = 4
LAST = 2
AHEAD = 2
EARLY = 2
EARLY_RUNS = 4
LATER_RUNS = 2
HALF_FIRST = 2

FLOPS = 2 * NPERM * C * C * H


def tile_permutatedsoftsparse_b_kernel(tc, weight, sparse_mask, s1, s0, rp, offs, out):
    nc = tc.nc
    with (
        tc.tile_pool(name="held", bufs=1) as held,
        tc.tile_pool(name="rows_in", bufs=1) as rows_in,
        tc.tile_pool(name="work", bufs=AHEAD + 1) as work,
        tc.tile_pool(name="results", bufs=RB) as results,
        tc.psum_pool(name="psum", bufs=BANKS) as psum,
    ):
        def paced(cb):
            return 0 < cb < CB - 1

        def v_tile(t, cb):
            if t == 0 and paced(cb):
                return rows_in.tile([P, PART], BF16, name=f"v{t}_{cb}", offset=(cb + 1) * S * F32_BYTES)
            return held.tile([P, PART], BF16, name=f"v{t}_{cb}")

        offsets = held.tile([P, N // 16], U16, name="offsets")
        nc.sync.dma_start(offsets[:], offs)
        s1_all = held.tile([P, N], F32, name="s1_all")
        s0_cols = held.tile([P, RB, NPERM], F32, name="s0_cols")
        rp_rows = [held.tile([P, NPERM, C], BF16, name=f"rp_rows{cb}") for cb in range(CB)]
        logits = [rows_in.tile([P, S], F32, name=f"logits{cb}", offset=cb * S * F32_BYTES) for cb in range(CB)]
        sw = [held.tile([P, S], F32, name=f"sw{cb}") for cb in range(CB)]
        prod = held.tile([P, K, PART], F32, name="prod")
        v = [[v_tile(t, cb) for cb in range(CB)] for t in range(PASSES)]

        def runs_of(count):
            return [slice(i * S // count, (i + 1) * S // count) for i in range(count)]

        def load_rows(cb):
            rows = slice(cb * P, (cb + 1) * P)
            for cols in runs_of(EARLY_RUNS if cb < EARLY else 1):
                nc.sync.dma_start(logits[cb][:, cols], sparse_mask[rows, cols])
                nc.sync.dma_start(sw[cb][:, cols], weight[rows, cols])

        def load_rp(cb, p):
            nc.sync.dma_start(rp_rows[cb][:, p, :], rp[p, cb * P : (cb + 1) * P, :])

        def make_sw(cb):
            runs = runs_of(EARLY_RUNS if cb < EARLY else LATER_RUNS)
            gate = work.tile([P, S], F32, name="gate")
            for cols in runs:
                nc.scalar.activation(logits[cb][:, cols], logits[cb][:, cols], ACT.Sigmoid)
            for cols in runs:
                nc.scalar.activation(gate[:, cols], logits[cb][:, cols], ACT.Relu, bias=-0.1, scale=1.2)
            for cols in runs:
                nc.vector.scalar_tensor_tensor(sw[cb][:, cols], gate[:, cols], 1.0, sw[cb][:, cols], ALU.min, ALU.mult)

        def look_up(cb, t, after_first=None):
            for k in range(K):
                j = k * H + t * PART
                nc.vector.tensor_tensor(
                    prod[:, k, :],
                    sw[cb][:].indirect(offsets[:, j // 16 : (j + PART) // 16]),
                    s1_all[:, j : j + PART],
                    ALU.mult,
                )
                if k == 0 and after_first:
                    after_first()
                if k >= 2:
                    nc.vector.tensor_tensor(prod[:, k - 1, :], prod[:, k - 1, :], prod[:, k - 2, :], ALU.add)

        def finish_v(cb, t):
            nc.vector.tensor_tensor(v[t][cb][:], prod[:, K - 1, :], prod[:, K - 2, :], ALU.add)

        def permute(bank, rb, cb, t, perms=range(NPERM)):
            for p in perms:
                nc.tensor.matmul(
                    bank[:, p, :],
                    rp_rows[cb][:, p, rb * P : (rb + 1) * P],
                    v[t][cb][:],
                    start=(cb == 0 and p == 0),
                    stop=(cb == CB - 1 and p == NPERM - 1),
                )

        def store(total, rb, t):
            nc.sync.dma_start(out[rb * P : (rb + 1) * P, t * PART : (t + 1) * PART], total[:])

        def clear_bank(bank, rb):
            terms = results.tile([P, NPERM, PART], F32, name="terms")
            for p in range(NPERM):
                nc.scalar.activation(terms[:, p, :], bank[:, p, :], ACT.Copy, scale=s0_cols[:, rb, p : p + 1])
            return terms

        def add_pairs(terms):
            half = NPERM // 2
            pairs = results.tile([P, half, PART], F32, name="pairs")
            nc.vector.tensor_tensor(pairs[:], terms[:, :half, :], terms[:, half:, :], ALU.add)
            return pairs

        def add_pair(pairs):
            total = results.tile([P, PART], F32, name="total")
            nc.vector.tensor_tensor(total[:], pairs[:, 0, :], pairs[:, 1, :], ALU.add)
            return total

        def read_out(bank, rb, t):
            sums = results.tile([P, NPERM // 2, PART], F32, name="pairs")
            for i in range(2):
                nc.scalar.activation(sums[:, i, :], bank[:, i, :], ACT.Copy, scale=s0_cols[:, rb, i : i + 1])
            for i in range(2):
                p = i + 2
                nc.vector.scalar_tensor_tensor(
                    sums[:, i, :], bank[:, p, :], s0_cols[:, rb, p : p + 1], sums[:, i, :], ALU.mult, ALU.add
                )
            store(add_pair(sums), rb, t)

        def last_output_block():
            rb, t = RB - 1, PASSES - 1
            total = None
            for p in range(NPERM):
                bank = psum.tile([P, PART], BF16, name="last_bank", tag="bank")
                for cb in range(CB):
                    nc.tensor.matmul(
                        bank[:],
                        rp_rows[cb][:, p, rb * P : (rb + 1) * P],
                        v[t][cb][:],
                        start=(cb == 0),
                        stop=(cb == CB - 1),
                    )
                scale = s0_cols[:, rb, p : p + 1]
                more = results.tile([P, PART], F32, name="total")
                if p == 0:
                    nc.scalar.activation(more[:], bank[:], ACT.Copy, scale=scale)
                else:
                    nc.vector.scalar_tensor_tensor(more[:], bank[:], scale, total[:], ALU.mult, ALU.add)
                total = more
            store(total, rb, t)

        def open_banks(blocks):
            return [psum.tile([P, NPERM, PART], BF16, name="bank", tag="bank") for rb in range(blocks)]

        first_banks = open_banks(RB)
        load_rows(0)
        nc.sync.dma_start(s1_all[:], s1[0, :].partition_broadcast(P))
        for cb in range(1, AHEAD):
            load_rows(cb)
        load_rp(0, 0)
        make_sw(0)
        for cb in range(CB):
            if cb + AHEAD < CB:
                load_rows(cb + AHEAD)
            for p in range(1 if cb == 0 else 0, NPERM):
                load_rp(cb, p)
            look_up(cb, 0)
            if paced(cb):
                make_sw(cb + 1)
                finish_v(cb, 0)
            else:
                finish_v(cb, 0)
                if cb + 1 < CB:
                    make_sw(cb + 1)
            if cb < CB - 1:
                for p in range(NPERM):
                    for rb in range(RB):
                        permute(first_banks[rb], rb, cb, 0, [p])
            else:
                for rb in range(RB):
                    permute(first_banks[rb], rb, cb, 0)
        nc.sync.dma_start(s0_cols[:], s0.rearrange("(b p) q -> p b q", p=P))

        terms = [clear_bank(first_banks[rb], rb) for rb in range(RB)]

        second_banks = open_banks(RB - 1)
        for cb in range(CB):
            look_up(cb, 1, lambda: finish_v(cb - 1, 1) if cb > 0 else None)
        finish_v(CB - 1, 1)
        for cb in range(CB):
            if cb == HALF_FIRST - 1:
                for half in (range(RB // 2), range(RB // 2, RB - 1)):
                    for early in range(HALF_FIRST):
                        for rb in half:
                            permute(second_banks[rb], rb, early, 1)
            elif HALF_FIRST <= cb < CB - LAST:
                for rb in range(RB - 1):
                    permute(second_banks[rb], rb, cb, 1)
        pairs = add_pairs(terms[0])
        for rb in range(RB):
            next_pairs = add_pairs(terms[rb + 1]) if rb + 1 < RB else None
            store(add_pair(pairs), rb, 0)
            pairs = next_pairs
        for rb in range(RB - 1):
            for cb in range(CB - LAST, CB):
                permute(second_banks[rb], rb, cb, 1)
            read_out(second_banks[rb], rb, 1)
        last_output_block()
